import numpy as np
import ml_dtypes


def mxq(x, axis, fmt="e4m3"):
    dtype, down = {"e4m3": (ml_dtypes.float8_e4m3fn, 7), "e5m2": (ml_dtypes.float8_e5m2, 14)}[fmt]
    v = np.moveaxis(np.asarray(x, np.float32).astype(ml_dtypes.bfloat16).astype(np.float64), axis, -1)
    blocks = v.reshape(v.shape[:-1] + (-1, 32))
    amax = np.abs(blocks).max(-1, keepdims=True)
    byte = np.maximum(np.where(amax > 0, np.frexp(amax)[1] - 1 + 127, 0) - down, 1)
    scale = np.exp2(byte - 127.0)
    codes = (blocks / scale).astype(np.float32).astype(dtype).astype(np.float64)
    return np.moveaxis((codes * scale).reshape(v.shape), -1, axis)


WIDE = False


def mx_kscale(k):
    if not WIDE:
        return np.ones(k)
    levels = np.array([10, -10, 5, -5, 0])
    if k % 512:
        return np.exp2(np.random.permutation(np.resize(levels, k // 32))).repeat(32)
    a = np.empty((k // 512, 16))
    for p in range(k // 512):
        a[p, :8] = np.random.permutation(np.resize(levels, 8))
        for g in range(8):
            far = levels[np.abs(levels - a[p, g]) >= 10]
            a[p, g + 8] = far[np.random.randint(len(far))]
    return np.exp2(a.ravel()).repeat(32)


BF16 = ml_dtypes.bfloat16


def bf(x):
    return np.asarray(x, np.float32).astype(BF16)


def f64(x):
    return np.asarray(x).astype(np.float64)


B, K, N = 1024, 2048, 2048
EPS = 1e-5
GELU_C = 0.7978845608


def setup_inputs():
    s = mx_kscale(K)
    return {"x": bf(np.random.standard_normal((B, K)) * s),
            "weight": bf(np.random.standard_normal((K, N)) * np.sqrt(2.0 / K) / s[:, None]),
            "bn_gamma": bf(np.random.uniform(0.5, 1.5, N)),
            "bn_beta": bf(np.random.standard_normal(N) * 0.1),
            "bn_mean": bf(np.random.standard_normal(N) * 0.1),
            "bn_var": bf(np.random.uniform(0.5, 1.5, N))}


def core(x, weight, bn_gamma, bn_beta, bn_mean, bn_var):
    acc = mxq(f64(x), 1, "e4m3") @ mxq(f64(weight), 0, "e4m3")
    x_norm = (acc - f64(bn_mean)) / np.sqrt(f64(bn_var) + EPS)
    bn_out = f64(bn_gamma) * x_norm + f64(bn_beta)
    gelu = 0.5 * bn_out * (1.0 + np.tanh(GELU_C * (bn_out + 0.044715 * bn_out * bn_out * bn_out)))
    return np.maximum(gelu, 0.0)


def e4m3fn_bytes(y):
    return np.clip(np.asarray(y, np.float64), -448.0, 448.0).astype(np.float32).astype(ml_dtypes.float8_e4m3fn).view(np.uint8)


Y_SCALE = 160.0


def reference(x, weight, bn_gamma, bn_beta, bn_mean, bn_var):
    out = core(x, weight, bn_gamma, bn_beta, bn_mean, bn_var)
    return out, e4m3fn_bytes(out * Y_SCALE)

@@ -1,0 +1,301 @@
+from contextlib import ExitStack
+
+import concourse.mybir as mybir
+from concourse.masks import make_identity
+
+B, K, N = 1024, 2048, 2048
+FLOPS = 2 * B * K * N
+EPS = 1e-5
+Y_SCALE = 160.0
+
+F32 = mybir.dt.float32
+BF16 = mybir.dt.bfloat16
+U32 = mybir.dt.uint32
+U8 = mybir.dt.uint8
+FP8X4 = mybir.dt.float8_e4m3fn_x4
+FP8 = mybir.dt.float8_e4m3fn
+ACT = mybir.ActivationFunctionType
+ALU = mybir.AluOpType
+
+P = 128
+PASSES = 4
+CHUNKS = 4
+S_INTERLEAVES = ((0, 3), (1, 1))
+V_EVAC_FROM = 4
+WARM_FIRST = 10
+
+
+def tile_modelnew_kernel(tc, x, weight, bn_gamma, bn_beta, bn_mean, bn_var, out_0, out_1):
+    nc = tc.nc
+    with ExitStack() as ctx:
+        const = ctx.enter_context(tc.tile_pool(name="const", bufs=1))
+        raw = ctx.enter_context(tc.tile_pool(name="raw", bufs=16))
+        codes = ctx.enter_context(tc.tile_pool(name="codes", bufs=1))
+        xg_pool = ctx.enter_context(tc.tile_pool(name="xg", bufs=4))
+        wg_s = ctx.enter_context(tc.tile_pool(name="wg_s", bufs=3))
+        wg_v = ctx.enter_context(tc.tile_pool(name="wg_v", bufs=3))
+        gt_pool = ctx.enter_context(tc.tile_pool(name="gt", bufs=12))
+        o0_pool = ctx.enter_context(tc.tile_pool(name="o0", bufs=3))
+        o1_pool = ctx.enter_context(tc.tile_pool(name="o1", bufs=3))
+        ps_a = ctx.enter_context(tc.psum_pool(name="ps_a", bufs=4))
+        ps_b = ctx.enter_context(tc.psum_pool(name="ps_b", bufs=4))
+        ctx.enter_context(tc.manual_schedule())
+
+        warm = const.tile([P, 512], BF16, name="warm", tag="warm")
+        nc.gpsimd.memset(warm[:], 0.0)
+        bnraw = const.tile([P, P], BF16, name="bnraw", tag="bnraw")
+        nc.gpsimd.memset(bnraw[64:P, :], 0.0)
+        for v, vec in enumerate((bn_gamma, bn_beta, bn_mean, bn_var)):
+            nc.scalar.dma_start(out=bnraw[16 * v:16 * (v + 1), :], in_=vec.rearrange("(t p) -> t p", p=P))
+        xraw, wraw = {}, {}
+
+        def load_x(r):
+            t = raw.tile([P, K], BF16, name="xraw%d" % r, tag="raw")
+            nc.sync.dma_start(out=t[:], in_=x[P * r:P * (r + 1), :])
+            xraw[r] = t
+
+        def load_w(q, c):
+            t = raw.tile([P, 4, 512], BF16, name="wraw%d_%d" % (q, c), tag="raw")
+            nc.sync.dma_start(
+                out=t[:],
+                in_=weight[512 * c:512 * (c + 1), 512 * q:512 * (q + 1)].rearrange("(p j) w -> p j w", j=4),
+            )
+            wraw[(q, c)] = t
+
+        for r in range(4):
+            load_x(r)
+        load_w(0, 0)
+        for r in range(4, 8):
+            load_x(r)
+        for q in range(CHUNKS):
+            for c in range(PASSES):
+                if (q, c) != (0, 0):
+                    load_w(q, c)
+
+        def keep_warm(count):
+            for i in range(count):
+                t = ps_b.tile([P, 512], F32, name="warm_ps", tag="ps")
+                nc.tensor.matmul(out=t[:], lhsT=warm[:, 0:P], rhs=warm[:], start=True, stop=True)
+
+        keep_warm(WARM_FIRST)
+        ident = const.tile([P, P], F32, name="ident", tag="ident")
+        make_identity(nc, ident[:])
+        one = const.tile([P, 1], F32, name="one", tag="one")
+        nc.vector.memset(one[:], 1.0)
+        scratch = const.tile([P, 1], F32, name="scratch", tag="scratch")
+        nc.scalar.activation(out=scratch[:], in_=one[:], func=ACT.Sqrt)
+        ident_bf = const.tile([P, P], BF16, name="ident_bf", tag="ident_bf")
+        nc.vector.tensor_copy(out=ident_bf[:], in_=ident[:])
+        a_sb = const.tile([P, 16], F32, name="a_sb", tag="a_sb")
+        b_sb = const.tile([P, 16], F32, name="b_sb", tag="b_sb")
+
+        bnf = const.tile([P, 64], F32, name="bnf", tag="bnf")
+        var_eps = const.tile([P, 16], F32, name="var_eps", tag="var_eps")
+        std = const.tile([P, 16], F32, name="std", tag="std")
+
+        def bn_transpose():
+            bn_ps = ps_a.tile([P, P], BF16, name="bn_ps", tag="ps")
+            nc.tensor.transpose(bn_ps[:], bnraw[:], ident_bf[:])
+            nc.vector.tensor_copy(out=bnf[:], in_=bn_ps[:, 0:64])
+            nc.vector.tensor_scalar(out=var_eps[:], in0=bnf[:, 48:64], scalar1=EPS, scalar2=None, op0=ALU.add)
+
+        def bn_sqrt():
+            nc.scalar.activation(out=std[:], in_=var_eps[:], func=ACT.Sqrt)
+            nc.scalar.activation(out=scratch[:], in_=one[:], func=ACT.Gelu_apprx_tanh)
+
+        def bn_finish():
+            rstd = const.tile([P, 16], F32, name="rstd", tag="rstd")
+            nc.vector.reciprocal(out=rstd[:], in_=std[:])
+            nc.vector.tensor_tensor(out=a_sb[:], in0=bnf[:, 0:16], in1=rstd[:], op=ALU.mult)
+            mean_a = const.tile([P, 16], F32, name="mean_a", tag="mean_a")
+            nc.vector.tensor_tensor(out=mean_a[:], in0=bnf[:, 32:48], in1=a_sb[:], op=ALU.mult)
+            nc.vector.tensor_tensor(out=b_sb[:], in0=bnf[:, 16:32], in1=mean_a[:], op=ALU.subtract)
+
+        xc, xs, wc, ws = {}, {}, {}, {}
+        for h in range(2):
+            for g in range(PASSES):
+                xc[(h, g)] = codes.tile([P, 512], U32, name="xc%d_%d" % (h, g), tag="xc%d_%d" % (h, g), align_bytes=64)
+                xs[(h, g)] = codes.tile([P, 512], U8, name="xs%d_%d" % (h, g), tag="xs%d_%d" % (h, g), align_bytes=64)
+        for q in range(CHUNKS):
+            for c in range(PASSES):
+                wc[(q, c)] = codes.tile([P, 512], U32, name="wc%d_%d" % (q, c), tag="wc%d_%d" % (q, c), align_bytes=64)
+                ws[(q, c)] = codes.tile([P, 512], U8, name="ws%d_%d" % (q, c), tag="ws%d_%d" % (q, c), align_bytes=64)
+
+        xt_ps, xg, wg, acc, gt, tr_ps, o0, o1 = {}, {}, {}, {}, {}, {}, {}, {}
+
+        def x_transpose(p, g):
+            t = ps_a.tile([P, 4, P], F32, name="xt_ps", tag="ps")
+            for rr in range(2):
+                words = xraw[2 * p + rr][:].bitcast(F32)
+                for u in range(2):
+                    nc.tensor.transpose(t[:, 2 * rr + u, :], words[:, 256 * g + u:256 * (g + 1):2], ident[:])
+            xt_ps[(p, g)] = t
+
+        def x_evacuate(p, g):
+            t = xg_pool.tile([P, 1024], BF16, name="xg", tag="xg", align_bytes=64)
+            nc.scalar.copy(out=t[:].bitcast(F32).rearrange("p (a r u) -> p a r u", a=2, u=2),
+                           in_=xt_ps[(p, g)][:].rearrange("p (a u) r -> p a r u", u=2))
+            xg[(p, g)] = t
+
+        def x_quantize(p, g):
+            cols = slice(256 * (p % 2), 256 * (p % 2 + 1))
+            nc.vector.quantize_mx(out=xc[(p // 2, g)][:, cols].bitcast(FP8X4), scales=xs[(p // 2, g)][:, cols], in_=xg[(p, g)][:])
+
+        def w_interleave(q, c):
+            on_scalar = (q, c) in S_INTERLEAVES
+            pool = wg_s if on_scalar else wg_v
+            t = pool.tile([P, 512, 4], BF16, name="wg", tag="wg", align_bytes=64)
+            src = wraw[(q, c)][:].rearrange("p j w -> p w j")
+            if on_scalar:
+                nc.scalar.copy(out=t[:], in_=src)
+            else:
+                nc.vector.tensor_copy(out=t[:], in_=src)
+            wg[(q, c)] = t
+
+        def w_quantize(q, c):
+            nc.vector.quantize_mx(out=wc[(q, c)][:].bitcast(FP8X4), scales=ws[(q, c)][:], in_=wg[(q, c)][:].rearrange("p w j -> p (w j)"))
+
+        def w_prepare(q):
+            for c in range(PASSES):
+                if (q, c) not in S_INTERLEAVES:
+                    w_interleave(q, c)
+                if c > 0:
+                    w_quantize(q, c - 1)
+            w_quantize(q, PASSES - 1)
+
+        def tiles_of(u):
+            return [0, 1, 2, 3] if u[2] is None else [2 * u[2], 2 * u[2] + 1]
+
+        def mx(u, j, c):
+            q, h, s = u
+            cols = slice(0, 512) if s is None else slice(256 * s, 256 * (s + 1))
+            width = cols.stop - cols.start
+            if c == 0:
+                acc[(u, j)] = (ps_b if u == units[0] else ps_a).tile([P, width], F32, name="acc", tag="ps")
+            chan = slice(P * j, P * (j + 1))
+            nc.tensor.matmul_mx(
+                out=acc[(u, j)][:],
+                lhsT=wc[(q, c)][:, chan].bitcast(FP8X4),
+                lhsT_scale=ws[(q, c)][:, chan],
+                rhs=xc[(h, c)][:, cols].bitcast(FP8X4),
+                rhs_scale=xs[(h, c)][:, cols],
+                start=(c == 0),
+                stop=(c == PASSES - 1),
+            )
+
+        def matmuls(u):
+            for j in range(4):
+                for c in range(PASSES):
+                    mx(u, j, c)
+
+        def gelus(u):
+            width = P * len(tiles_of(u))
+            for j in range(4):
+                t = gt_pool.tile([P, width], F32, name="gt", tag="gt")
+                col = 4 * u[0] + j
+                nc.scalar.activation(out=t[:], in_=acc[(u, j)][:], func=ACT.Gelu_apprx_tanh,
+                                     bias=b_sb[:, col:col + 1], scale=a_sb[:, col:col + 1])
+                gt[(u, j)] = t
+
+        def back_transposes(u):
+            for l in range(len(tiles_of(u))):
+                t = ps_b.tile([P, 512], F32, name="tr_ps", tag="ps")
+                for j in range(4):
+                    nc.tensor.transpose(t[:, P * j:P * (j + 1)], gt[(u, j)][:, P * l:P * (l + 1)], ident[:])
+                tr_ps[(u, l)] = t
+
+        def evacuate(u, share_with_vector):
+            n = len(tiles_of(u))
+            o0[u] = o0_pool.tile([P, n, 512], F32, name="o0", tag="o0")
+            for l in range(n):
+                if share_with_vector and l % 2 == 1:
+                    nc.vector.tensor_scalar(out=o0[u][:, l, :], in0=tr_ps[(u, l)][:], scalar1=0.0, scalar2=None, op0=ALU.max)
+                else:
+                    nc.scalar.activation(out=o0[u][:, l, :], in_=tr_ps[(u, l)][:], func=ACT.Relu)
+
+        def cast_and_store(u):
+            q, h, s = u
+            tl = tiles_of(u)
+            n = len(tl)
+            o1[u] = o1_pool.tile([P, n, 512], FP8, name="o1", tag="o1")
+            row0 = 512 * h + P * tl[0]
+            chan = slice(512 * q, 512 * (q + 1))
+            for a in range(n // 2):
+                two = slice(2 * a, 2 * a + 2)
+                nc.vector.tensor_scalar(out=o1[u][:, two, :], in0=o0[u][:, two, :], scalar1=Y_SCALE, scalar2=None,
+                                        op0=ALU.mult, saturate=False)
+                rows = slice(row0 + 256 * a, row0 + 256 * (a + 1))
+                nc.sync.dma_start(out=out_0[rows, chan].rearrange("(t p) n -> p t n", p=P), in_=o0[u][:, two, :])
+            nc.sync.dma_start(out=out_1[row0:row0 + P * n, chan].rearrange("(t p) n -> p t n", p=P),
+                              in_=o1[u][:].bitcast(U8))
+
+        units = [(q, h, None) for q in range(CHUNKS) for h in range(2)][:-1] + [(3, 1, 0), (3, 1, 1)]
+        u0, u1 = units[0], units[1]
+        for p in range(4):
+            if p == 3:
+                mx(u0, 0, 0)
+                mx(u0, 1, 0)
+            x_transpose(p, 0)
+            if p == 0:
+                bn_transpose()
+            x_transpose(p, 1)
+            if p == 3:
+                mx(u0, 2, 0)
+                mx(u0, 3, 0)
+            else:
+                keep_warm(2)
+            x_transpose(p, 2)
+            x_transpose(p, 3)
+            if p < 2:
+                keep_warm(2)
+            for g in range(PASSES):
+                x_evacuate(p, g)
+                if (p, g) == (1, 1):
+                    bn_sqrt()
+            if p < 3:
+                for g in range(PASSES):
+                    if (p, g) == (0, 3):
+                        w_interleave(0, 0)
+                    if (p, g) == (1, 2):
+                        bn_finish()
+                    x_quantize(p, g)
+            if p == 0:
+                w_quantize(0, 0)
+        for (q, c) in S_INTERLEAVES:
+            w_interleave(q, c)
+        for c in range(PASSES):
+            if 0 < c < 3:
+                w_interleave(0, c)
+            x_quantize(3, c)
+            if c > 0:
+                w_quantize(0, c)
+                for j in range(4):
+                    mx(u0, j, c)
+            for j in range(4):
+                mx(u1, j, c)
+        gelus(u0)
+        gelus(u1)
+        w_prepare(1)
+        back_transposes(units[0])
+        evacuate(units[0], False)
+        pending = [units[0]]
+        next_chunk = 2
+        for i in range(2, len(units)):
+            matmuls(units[i])
+            gelus(units[i])
+            back_transposes(units[i - 1])
+            evacuate(units[i - 1], i - 1 >= V_EVAC_FROM)
+            pending.append(units[i - 1])
+            if units[i][1] == 0 and next_chunk < CHUNKS:
+                w_prepare(next_chunk)
+                next_chunk += 1
+                flush = True
+            else:
+                flush = next_chunk == CHUNKS
+            if flush:
+                for u in pending:
+                    cast_and_store(u)
+                pending.clear()
+        back_transposes(units[-1])
+        evacuate(units[-1], True)
+        cast_and_store(units[-1])

@@ -145,11 +145,12 @@ def tile_modelnew_kernel(tc, x, weight, bn_gamma, bn_beta, bn_mean, bn_var, out_
             on_scalar = (q, c) in S_INTERLEAVES
             pool = wg_s if on_scalar else wg_v
             t = pool.tile([P, 512, 4], BF16, name="wg", tag="wg", align_bytes=64)
-            src = wraw[(q, c)][:].rearrange("p j w -> p w j")
+            src = wraw[(q, c)][:].rearrange("p j (c i) -> p c j i", i=4)
+            dst = t[:].rearrange("p (c i) j -> p c j i", i=4)
             if on_scalar:
-                nc.scalar.copy(out=t[:], in_=src)
+                nc.scalar.copy(out=dst, in_=src)
             else:
-                nc.vector.tensor_copy(out=t[:], in_=src)
+                nc.vector.tensor_copy(out=dst, in_=src)
             wg[(q, c)] = t
 
         def w_quantize(q, c):

@@ -83,7 +83,7 @@ def tile_modelnew_kernel(tc, x, weight, bn_gamma, bn_beta, bn_mean, bn_var, out_
         one = const.tile([P, 1], F32, name="one", tag="one")
         nc.vector.memset(one[:], 1.0)
         scratch = const.tile([P, 1], F32, name="scratch", tag="scratch")
-        nc.scalar.activation(out=scratch[:], in_=one[:], func=ACT.Sqrt)
+        nc.scalar.activation(out=scratch[:], in_=one[:], func=ACT.Gelu_apprx_tanh)
         ident_bf = const.tile([P, P], BF16, name="ident_bf", tag="ident_bf")
         nc.vector.tensor_copy(out=ident_bf[:], in_=ident[:])
         a_sb = const.tile([P, 16], F32, name="a_sb", tag="a_sb")
@@ -91,25 +91,20 @@ def tile_modelnew_kernel(tc, x, weight, bn_gamma, bn_beta, bn_mean, bn_var, out_
 
         bnf = const.tile([P, 64], F32, name="bnf", tag="bnf")
         var_eps = const.tile([P, 16], F32, name="var_eps", tag="var_eps")
-        std = const.tile([P, 16], F32, name="std", tag="std")
+        neg_half = const.tile([P, 16], F32, name="neg_half", tag="neg_half")
+        nc.gpsimd.memset(neg_half[:], -0.5)
 
         def bn_transpose():
             bn_ps = ps_a.tile([P, P], BF16, name="bn_ps", tag="ps")
             nc.tensor.transpose(bn_ps[:], bnraw[:], ident_bf[:])
             nc.vector.tensor_copy(out=bnf[:], in_=bn_ps[:, 0:64])
-            nc.vector.tensor_scalar(out=var_eps[:], in0=bnf[:, 48:64], scalar1=EPS, scalar2=None, op0=ALU.add)
-
-        def bn_sqrt():
-            nc.scalar.activation(out=std[:], in_=var_eps[:], func=ACT.Sqrt)
-            nc.scalar.activation(out=scratch[:], in_=one[:], func=ACT.Gelu_apprx_tanh)
-
-        def bn_finish():
+            nc.gpsimd.tensor_scalar(out=var_eps[:], in0=bnf[:, 48:64], scalar1=EPS, scalar2=None, op0=ALU.add)
             rstd = const.tile([P, 16], F32, name="rstd", tag="rstd")
-            nc.vector.reciprocal(out=rstd[:], in_=std[:])
-            nc.vector.tensor_tensor(out=a_sb[:], in0=bnf[:, 0:16], in1=rstd[:], op=ALU.mult)
+            nc.gpsimd.tensor_tensor(out=rstd[:], in0=var_eps[:], in1=neg_half[:], op=ALU.pow)
+            nc.gpsimd.tensor_tensor(out=a_sb[:], in0=bnf[:, 0:16], in1=rstd[:], op=ALU.mult)
             mean_a = const.tile([P, 16], F32, name="mean_a", tag="mean_a")
-            nc.vector.tensor_tensor(out=mean_a[:], in0=bnf[:, 32:48], in1=a_sb[:], op=ALU.mult)
-            nc.vector.tensor_tensor(out=b_sb[:], in0=bnf[:, 16:32], in1=mean_a[:], op=ALU.subtract)
+            nc.gpsimd.tensor_tensor(out=mean_a[:], in0=bnf[:, 32:48], in1=a_sb[:], op=ALU.mult)
+            nc.gpsimd.tensor_tensor(out=b_sb[:], in0=bnf[:, 16:32], in1=mean_a[:], op=ALU.subtract)
 
         xc, xs, wc, ws = {}, {}, {}, {}
         for h in range(2):
@@ -251,14 +246,10 @@ def tile_modelnew_kernel(tc, x, weight, bn_gamma, bn_beta, bn_mean, bn_var, out_
                 keep_warm(2)
             for g in range(PASSES):
                 x_evacuate(p, g)
-                if (p, g) == (1, 1):
-                    bn_sqrt()
             if p < 3:
                 for g in range(PASSES):
                     if (p, g) == (0, 3):
                         w_interleave(0, 0)
-                    if (p, g) == (1, 2):
-                        bn_finish()
                     x_quantize(p, g)
             if p == 0:
                 w_quantize(0, 0)

@@ -37,6 +37,7 @@ def tile_modelnew_kernel(tc, x, weight, bn_gamma, bn_beta, bn_mean, bn_var, out_
         gt_pool = ctx.enter_context(tc.tile_pool(name="gt", bufs=12))
         o0_pool = ctx.enter_context(tc.tile_pool(name="o0", bufs=3))
         o1_pool = ctx.enter_context(tc.tile_pool(name="o1", bufs=3))
+        end_pool = ctx.enter_context(tc.tile_pool(name="end", bufs=1))
         ps_a = ctx.enter_context(tc.psum_pool(name="ps_a", bufs=4))
         ps_b = ctx.enter_context(tc.psum_pool(name="ps_b", bufs=4))
         ctx.enter_context(tc.manual_schedule())
@@ -160,11 +161,11 @@ def tile_modelnew_kernel(tc, x, weight, bn_gamma, bn_beta, bn_mean, bn_var, out_
             w_quantize(q, PASSES - 1)
 
         def tiles_of(u):
-            return [0, 1, 2, 3] if u[2] is None else [2 * u[2], 2 * u[2] + 1]
+            return [0, 1, 2, 3] if u[2] is None else list(range(u[2][0], u[2][0] + u[2][1]))
 
         def mx(u, j, c):
             q, h, s = u
-            cols = slice(0, 512) if s is None else slice(256 * s, 256 * (s + 1))
+            cols = slice(P * tiles_of(u)[0], P * (tiles_of(u)[-1] + 1))
             width = cols.stop - cols.start
             if c == 0:
                 acc[(u, j)] = (ps_b if u == units[0] else ps_a).tile([P, width], F32, name="acc", tag="ps")
@@ -225,7 +226,27 @@ def tile_modelnew_kernel(tc, x, weight, bn_gamma, bn_beta, bn_mean, bn_var, out_
             nc.sync.dma_start(out=out_1[row0:row0 + P * n, chan].rearrange("(t p) n -> p t n", p=P),
                               in_=o1[u][:].bitcast(U8))
 
-        units = [(q, h, None) for q in range(CHUNKS) for h in range(2)][:-1] + [(3, 1, 0), (3, 1, 1)]
+        def finish_small(u):
+            q, h, s = u
+            o0[u] = end_pool.tile([P, 1, 512], F32, name="o0_end%d" % tiles_of(u)[0], tag="o0_end%d" % tiles_of(u)[0])
+            o1[u] = end_pool.tile([P, 1, 512], FP8, name="o1_end%d" % tiles_of(u)[0], tag="o1_end%d" % tiles_of(u)[0])
+            row0 = 512 * h + P * tiles_of(u)[0]
+            chan = slice(512 * q, 512 * (q + 1))
+            banks = []
+            for half in range(2):
+                t = ps_b.tile([P, 256], F32, name="tr_ps", tag="ps")
+                for j in (2 * half, 2 * half + 1):
+                    nc.tensor.transpose(t[:, P * (j % 2):P * (j % 2 + 1)], gt[(u, j)][:], ident[:])
+                banks.append(t)
+            nc.vector.tensor_scalar(out=o0[u][:, 0, 0:256], in0=banks[0][:], scalar1=0.0, scalar2=None, op0=ALU.max)
+            nc.scalar.activation(out=o0[u][:, 0, 256:512], in_=banks[1][:], func=ACT.Relu)
+            nc.sync.dma_start(out=out_0[row0:row0 + P, chan], in_=o0[u][:, 0, :])
+            nc.vector.tensor_scalar(out=o1[u][:, 0, 0:256], in0=o0[u][:, 0, 0:256], scalar1=Y_SCALE, scalar2=None,
+                                    op0=ALU.mult, saturate=False)
+            nc.scalar.activation(out=o1[u][:, 0, 256:512], in_=o0[u][:, 0, 256:512], func=ACT.Copy, scale=Y_SCALE, saturate=False)
+            nc.sync.dma_start(out=out_1[row0:row0 + P, chan], in_=o1[u][:, 0, :].bitcast(U8))
+
+        units = [(q, h, None) for q in range(CHUNKS) for h in range(2)][:-1] + [(3, 1, (0, 2)), (3, 1, (2, 1)), (3, 1, (3, 1))]
         u0, u1 = units[0], units[1]
         for p in range(4):
             if p == 3:
@@ -272,7 +293,7 @@ def tile_modelnew_kernel(tc, x, weight, bn_gamma, bn_beta, bn_mean, bn_var, out_
         evacuate(units[0], False)
         pending = [units[0]]
         next_chunk = 2
-        for i in range(2, len(units)):
+        for i in range(2, len(units) - 2):
             matmuls(units[i])
             gelus(units[i])
             back_transposes(units[i - 1])
@@ -288,6 +309,12 @@ def tile_modelnew_kernel(tc, x, weight, bn_gamma, bn_beta, bn_mean, bn_var, out_
                 for u in pending:
                     cast_and_store(u)
                 pending.clear()
-        back_transposes(units[-1])
-        evacuate(units[-1], True)
-        cast_and_store(units[-1])
+        back_transposes(units[-3])
+        evacuate(units[-3], True)
+        cast_and_store(units[-3])
+        matmuls(units[-2])
+        gelus(units[-2])
+        matmuls(units[-1])
+        gelus(units[-1])
+        finish_small(units[-2])
+        finish_small(units[-1])

@@ -141,8 +141,8 @@ def tile_modelnew_kernel(tc, x, weight, bn_gamma, bn_beta, bn_mean, bn_var, out_
             on_scalar = (q, c) in S_INTERLEAVES
             pool = wg_s if on_scalar else wg_v
             t = pool.tile([P, 512, 4], BF16, name="wg", tag="wg", align_bytes=64)
-            src = wraw[(q, c)][:].rearrange("p j (c i) -> p c j i", i=4)
-            dst = t[:].rearrange("p (c i) j -> p c j i", i=4)
+            src = wraw[(q, c)][:].rearrange("p j (c i) -> p c j i", i=8)
+            dst = t[:].rearrange("p (c i) j -> p c j i", i=8)
             if on_scalar:
                 nc.scalar.copy(out=dst, in_=src)
             else:

@@ -23,6 +23,7 @@ CHUNKS = 4
 S_INTERLEAVES = ((0, 3), (1, 1))
 V_EVAC_FROM = 4
 WARM_FIRST = 10
+SHIFT = 128
 
 
 def tile_modelnew_kernel(tc, x, weight, bn_gamma, bn_beta, bn_mean, bn_var, out_0, out_1):
@@ -111,11 +112,11 @@ def tile_modelnew_kernel(tc, x, weight, bn_gamma, bn_beta, bn_mean, bn_var, out_
         for h in range(2):
             for g in range(PASSES):
                 xc[(h, g)] = codes.tile([P, 512], U32, name="xc%d_%d" % (h, g), tag="xc%d_%d" % (h, g), align_bytes=64)
-                xs[(h, g)] = codes.tile([P, 512], U8, name="xs%d_%d" % (h, g), tag="xs%d_%d" % (h, g), align_bytes=64)
+                xs[(h, g)] = codes.tile([P, 768], U8, name="xs%d_%d" % (h, g), tag="xs%d_%d" % (h, g), align_bytes=64)[:, SHIFT:SHIFT + 512]
         for q in range(CHUNKS):
             for c in range(PASSES):
                 wc[(q, c)] = codes.tile([P, 512], U32, name="wc%d_%d" % (q, c), tag="wc%d_%d" % (q, c), align_bytes=64)
-                ws[(q, c)] = codes.tile([P, 512], U8, name="ws%d_%d" % (q, c), tag="ws%d_%d" % (q, c), align_bytes=64)
+                ws[(q, c)] = codes.tile([P, 768], U8, name="ws%d_%d" % (q, c), tag="ws%d_%d" % (q, c), align_bytes=64)[:, SHIFT:SHIFT + 512]
 
         xt_ps, xg, wg, acc, gt, tr_ps, o0, o1 = {}, {}, {}, {}, {}, {}, {}, {}
 

from contextlib import ExitStack

import concourse.mybir as mybir
from concourse.masks import make_identity

B, K, N = 1024, 2048, 2048
FLOPS = 2 * B * K * N
EPS = 1e-5
Y_SCALE = 160.0

F32 = mybir.dt.float32
BF16 = mybir.dt.bfloat16
U32 = mybir.dt.uint32
U8 = mybir.dt.uint8
FP8X4 = mybir.dt.float8_e4m3fn_x4
FP8 = mybir.dt.float8_e4m3fn
ACT = mybir.ActivationFunctionType
ALU = mybir.AluOpType

P = 128
PASSES = 4
CHUNKS = 4
S_INTERLEAVES = ((0, 3), (1, 1))
V_EVAC_FROM = 4
WARM_FIRST = 10
SHIFT = 128


def tile_modelnew_kernel(tc, x, weight, bn_gamma, bn_beta, bn_mean, bn_var, out_0, out_1):
    nc = tc.nc
    with ExitStack() as ctx:
        const = ctx.enter_context(tc.tile_pool(name="const", bufs=1))
        raw = ctx.enter_context(tc.tile_pool(name="raw", bufs=16))
        codes = ctx.enter_context(tc.tile_pool(name="codes", bufs=1))
        xg_pool = ctx.enter_context(tc.tile_pool(name="xg", bufs=4))
        wg_s = ctx.enter_context(tc.tile_pool(name="wg_s", bufs=3))
        wg_v = ctx.enter_context(tc.tile_pool(name="wg_v", bufs=3))
        gt_pool = ctx.enter_context(tc.tile_pool(name="gt", bufs=12))
        o0_pool = ctx.enter_context(tc.tile_pool(name="o0", bufs=3))
        o1_pool = ctx.enter_context(tc.tile_pool(name="o1", bufs=3))
        end_pool = ctx.enter_context(tc.tile_pool(name="end", bufs=1))
        ps_a = ctx.enter_context(tc.psum_pool(name="ps_a", bufs=4))
        ps_b = ctx.enter_context(tc.psum_pool(name="ps_b", bufs=4))
        ctx.enter_context(tc.manual_schedule())

        warm = const.tile([P, 512], BF16, name="warm", tag="warm")
        nc.gpsimd.memset(warm[:], 0.0)
        bnraw = const.tile([P, P], BF16, name="bnraw", tag="bnraw")
        nc.gpsimd.memset(bnraw[64:P, :], 0.0)
        for v, vec in enumerate((bn_gamma, bn_beta, bn_mean, bn_var)):
            nc.scalar.dma_start(out=bnraw[16 * v:16 * (v + 1), :], in_=vec.rearrange("(t p) -> t p", p=P))
        xraw, wraw = {}, {}

        def load_x(r):
            t = raw.tile([P, K], BF16, name="xraw%d" % r, tag="raw")
            nc.sync.dma_start(out=t[:], in_=x[P * r:P * (r + 1), :])
            xraw[r] = t

        def load_w(q, c):
            t = raw.tile([P, 4, 512], BF16, name="wraw%d_%d" % (q, c), tag="raw")
            nc.sync.dma_start(
                out=t[:],
                in_=weight[512 * c:512 * (c + 1), 512 * q:512 * (q + 1)].rearrange("(p j) w -> p j w", j=4),
            )
            wraw[(q, c)] = t

        for r in range(4):
            load_x(r)
        load_w(0, 0)
        for r in range(4, 8):
            load_x(r)
        for q in range(CHUNKS):
            for c in range(PASSES):
                if (q, c) != (0, 0):
                    load_w(q, c)

        def keep_warm(count):
            for i in range(count):
                t = ps_b.tile([P, 512], F32, name="warm_ps", tag="ps")
                nc.tensor.matmul(out=t[:], lhsT=warm[:, 0:P], rhs=warm[:], start=True, stop=True)

        keep_warm(WARM_FIRST)
        ident = const.tile([P, P], F32, name="ident", tag="ident")
        make_identity(nc, ident[:])
        one = const.tile([P, 1], F32, name="one", tag="one")
        nc.vector.memset(one[:], 1.0)
        scratch = const.tile([P, 1], F32, name="scratch", tag="scratch")
        nc.scalar.activation(out=scratch[:], in_=one[:], func=ACT.Gelu_apprx_tanh)
        ident_bf = const.tile([P, P], BF16, name="ident_bf", tag="ident_bf")
        nc.vector.tensor_copy(out=ident_bf[:], in_=ident[:])
        a_sb = const.tile([P, 16], F32, name="a_sb", tag="a_sb")
        b_sb = const.tile([P, 16], F32, name="b_sb", tag="b_sb")

        bnf = const.tile([P, 64], F32, name="bnf", tag="bnf")
        var_eps = const.tile([P, 16], F32, name="var_eps", tag="var_eps")
        neg_half = const.tile([P, 16], F32, name="neg_half", tag="neg_half")
        nc.gpsimd.memset(neg_half[:], -0.5)

        def bn_transpose():
            bn_ps = ps_a.tile([P, P], BF16, name="bn_ps", tag="ps")
            nc.tensor.transpose(bn_ps[:], bnraw[:], ident_bf[:])
            nc.vector.tensor_copy(out=bnf[:], in_=bn_ps[:, 0:64])
            nc.gpsimd.tensor_scalar(out=var_eps[:], in0=bnf[:, 48:64], scalar1=EPS, scalar2=None, op0=ALU.add)
            rstd = const.tile([P, 16], F32, name="rstd", tag="rstd")
            nc.gpsimd.tensor_tensor(out=rstd[:], in0=var_eps[:], in1=neg_half[:], op=ALU.pow)
            nc.gpsimd.tensor_tensor(out=a_sb[:], in0=bnf[:, 0:16], in1=rstd[:], op=ALU.mult)
            mean_a = const.tile([P, 16], F32, name="mean_a", tag="mean_a")
            nc.gpsimd.tensor_tensor(out=mean_a[:], in0=bnf[:, 32:48], in1=a_sb[:], op=ALU.mult)
            nc.gpsimd.tensor_tensor(out=b_sb[:], in0=bnf[:, 16:32], in1=mean_a[:], op=ALU.subtract)

        xc, xs, wc, ws = {}, {}, {}, {}
        for h in range(2):
            for g in range(PASSES):
                xc[(h, g)] = codes.tile([P, 512], U32, name="xc%d_%d" % (h, g), tag="xc%d_%d" % (h, g), align_bytes=64)
                xs[(h, g)] = codes.tile([P, 768], U8, name="xs%d_%d" % (h, g), tag="xs%d_%d" % (h, g), align_bytes=64)[:, SHIFT:SHIFT + 512]
        for q in range(CHUNKS):
            for c in range(PASSES):
                wc[(q, c)] = codes.tile([P, 512], U32, name="wc%d_%d" % (q, c), tag="wc%d_%d" % (q, c), align_bytes=64)
                ws[(q, c)] = codes.tile([P, 768], U8, name="ws%d_%d" % (q, c), tag="ws%d_%d" % (q, c), align_bytes=64)[:, SHIFT:SHIFT + 512]

        xt_ps, xg, wg, acc, gt, tr_ps, o0, o1 = {}, {}, {}, {}, {}, {}, {}, {}

        def x_transpose(p, g):
            t = ps_a.tile([P, 4, P], F32, name="xt_ps", tag="ps")
            for rr in range(2):
                words = xraw[2 * p + rr][:].bitcast(F32)
                for u in range(2):
                    nc.tensor.transpose(t[:, 2 * rr + u, :], words[:, 256 * g + u:256 * (g + 1):2], ident[:])
            xt_ps[(p, g)] = t

        def x_evacuate(p, g):
            t = xg_pool.tile([P, 1024], BF16, name="xg", tag="xg", align_bytes=64)
            nc.scalar.copy(out=t[:].bitcast(F32).rearrange("p (a r u) -> p a r u", a=2, u=2),
                           in_=xt_ps[(p, g)][:].rearrange("p (a u) r -> p a r u", u=2))
            xg[(p, g)] = t

        def x_quantize(p, g):
            cols = slice(256 * (p % 2), 256 * (p % 2 + 1))
            nc.vector.quantize_mx(out=xc[(p // 2, g)][:, cols].bitcast(FP8X4), scales=xs[(p // 2, g)][:, cols], in_=xg[(p, g)][:])

        def w_interleave(q, c):
            on_scalar = (q, c) in S_INTERLEAVES
            pool = wg_s if on_scalar else wg_v
            t = pool.tile([P, 512, 4], BF16, name="wg", tag="wg", align_bytes=64)
            src = wraw[(q, c)][:].rearrange("p j (c i) -> p c j i", i=8)
            dst = t[:].rearrange("p (c i) j -> p c j i", i=8)
            if on_scalar:
                nc.scalar.copy(out=dst, in_=src)
            else:
                nc.vector.tensor_copy(out=dst, in_=src)
            wg[(q, c)] = t

        def w_quantize(q, c):
            nc.vector.quantize_mx(out=wc[(q, c)][:].bitcast(FP8X4), scales=ws[(q, c)][:], in_=wg[(q, c)][:].rearrange("p w j -> p (w j)"))

        def w_prepare(q):
            for c in range(PASSES):
                if (q, c) not in S_INTERLEAVES:
                    w_interleave(q, c)
                if c > 0:
                    w_quantize(q, c - 1)
            w_quantize(q, PASSES - 1)

        def tiles_of(u):
            return [0, 1, 2, 3] if u[2] is None else list(range(u[2][0], u[2][0] + u[2][1]))

        def mx(u, j, c):
            q, h, s = u
            cols = slice(P * tiles_of(u)[0], P * (tiles_of(u)[-1] + 1))
            width = cols.stop - cols.start
            if c == 0:
                acc[(u, j)] = (ps_b if u == units[0] else ps_a).tile([P, width], F32, name="acc", tag="ps")
            chan = slice(P * j, P * (j + 1))
            nc.tensor.matmul_mx(
                out=acc[(u, j)][:],
                lhsT=wc[(q, c)][:, chan].bitcast(FP8X4),
                lhsT_scale=ws[(q, c)][:, chan],
                rhs=xc[(h, c)][:, cols].bitcast(FP8X4),
                rhs_scale=xs[(h, c)][:, cols],
                start=(c == 0),
                stop=(c == PASSES - 1),
            )

        def matmuls(u):
            for j in range(4):
                for c in range(PASSES):
                    mx(u, j, c)

        def gelus(u):
            width = P * len(tiles_of(u))
            for j in range(4):
                t = gt_pool.tile([P, width], F32, name="gt", tag="gt")
                col = 4 * u[0] + j
                nc.scalar.activation(out=t[:], in_=acc[(u, j)][:], func=ACT.Gelu_apprx_tanh,
                                     bias=b_sb[:, col:col + 1], scale=a_sb[:, col:col + 1])
                gt[(u, j)] = t

        def back_transposes(u):
            for l in range(len(tiles_of(u))):
                t = ps_b.tile([P, 512], F32, name="tr_ps", tag="ps")
                for j in range(4):
                    nc.tensor.transpose(t[:, P * j:P * (j + 1)], gt[(u, j)][:, P * l:P * (l + 1)], ident[:])
                tr_ps[(u, l)] = t

        def evacuate(u, share_with_vector):
            n = len(tiles_of(u))
            o0[u] = o0_pool.tile([P, n, 512], F32, name="o0", tag="o0")
            for l in range(n):
                if share_with_vector and l % 2 == 1:
                    nc.vector.tensor_scalar(out=o0[u][:, l, :], in0=tr_ps[(u, l)][:], scalar1=0.0, scalar2=None, op0=ALU.max)
                else:
                    nc.scalar.activation(out=o0[u][:, l, :], in_=tr_ps[(u, l)][:], func=ACT.Relu)

        def cast_and_store(u):
            q, h, s = u
            tl = tiles_of(u)
            n = len(tl)
            o1[u] = o1_pool.tile([P, n, 512], FP8, name="o1", tag="o1")
            row0 = 512 * h + P * tl[0]
            chan = slice(512 * q, 512 * (q + 1))
            for a in range(n // 2):
                two = slice(2 * a, 2 * a + 2)
                nc.vector.tensor_scalar(out=o1[u][:, two, :], in0=o0[u][:, two, :], scalar1=Y_SCALE, scalar2=None,
                                        op0=ALU.mult, saturate=False)
                rows = slice(row0 + 256 * a, row0 + 256 * (a + 1))
                nc.sync.dma_start(out=out_0[rows, chan].rearrange("(t p) n -> p t n", p=P), in_=o0[u][:, two, :])
            nc.sync.dma_start(out=out_1[row0:row0 + P * n, chan].rearrange("(t p) n -> p t n", p=P),
                              in_=o1[u][:].bitcast(U8))

        def finish_small(u):
            q, h, s = u
            o0[u] = end_pool.tile([P, 1, 512], F32, name="o0_end%d" % tiles_of(u)[0], tag="o0_end%d" % tiles_of(u)[0])
            o1[u] = end_pool.tile([P, 1, 512], FP8, name="o1_end%d" % tiles_of(u)[0], tag="o1_end%d" % tiles_of(u)[0])
            row0 = 512 * h + P * tiles_of(u)[0]
            chan = slice(512 * q, 512 * (q + 1))
            banks = []
            for half in range(2):
                t = ps_b.tile([P, 256], F32, name="tr_ps", tag="ps")
                for j in (2 * half, 2 * half + 1):
                    nc.tensor.transpose(t[:, P * (j % 2):P * (j % 2 + 1)], gt[(u, j)][:], ident[:])
                banks.append(t)
            nc.vector.tensor_scalar(out=o0[u][:, 0, 0:256], in0=banks[0][:], scalar1=0.0, scalar2=None, op0=ALU.max)
            nc.scalar.activation(out=o0[u][:, 0, 256:512], in_=banks[1][:], func=ACT.Relu)
            nc.sync.dma_start(out=out_0[row0:row0 + P, chan], in_=o0[u][:, 0, :])
            nc.vector.tensor_scalar(out=o1[u][:, 0, 0:256], in0=o0[u][:, 0, 0:256], scalar1=Y_SCALE, scalar2=None,
                                    op0=ALU.mult, saturate=False)
            nc.scalar.activation(out=o1[u][:, 0, 256:512], in_=o0[u][:, 0, 256:512], func=ACT.Copy, scale=Y_SCALE, saturate=False)
            nc.sync.dma_start(out=out_1[row0:row0 + P, chan], in_=o1[u][:, 0, :].bitcast(U8))

        units = [(q, h, None) for q in range(CHUNKS) for h in range(2)][:-1] + [(3, 1, (0, 2)), (3, 1, (2, 1)), (3, 1, (3, 1))]
        u0, u1 = units[0], units[1]
        for p in range(4):
            if p == 3:
                mx(u0, 0, 0)
                mx(u0, 1, 0)
            x_transpose(p, 0)
            if p == 0:
                bn_transpose()
            x_transpose(p, 1)
            if p == 3:
                mx(u0, 2, 0)
                mx(u0, 3, 0)
            else:
                keep_warm(2)
            x_transpose(p, 2)
            x_transpose(p, 3)
            if p < 2:
                keep_warm(2)
            for g in range(PASSES):
                x_evacuate(p, g)
            if p < 3:
                for g in range(PASSES):
                    if (p, g) == (0, 3):
                        w_interleave(0, 0)
                    x_quantize(p, g)
            if p == 0:
                w_quantize(0, 0)
        for (q, c) in S_INTERLEAVES:
            w_interleave(q, c)
        for c in range(PASSES):
            if 0 < c < 3:
                w_interleave(0, c)
            x_quantize(3, c)
            if c > 0:
                w_quantize(0, c)
                for j in range(4):
                    mx(u0, j, c)
            for j in range(4):
                mx(u1, j, c)
        gelus(u0)
        gelus(u1)
        w_prepare(1)
        back_transposes(units[0])
        evacuate(units[0], False)
        pending = [units[0]]
        next_chunk = 2
        for i in range(2, len(units) - 2):
            matmuls(units[i])
            gelus(units[i])
            back_transposes(units[i - 1])
            evacuate(units[i - 1], i - 1 >= V_EVAC_FROM)
            pending.append(units[i - 1])
            if units[i][1] == 0 and next_chunk < CHUNKS:
                w_prepare(next_chunk)
                next_chunk += 1
                flush = True
            else:
                flush = next_chunk == CHUNKS
            if flush:
                for u in pending:
                    cast_and_store(u)
                pending.clear()
        back_transposes(units[-3])
        evacuate(units[-3], True)
        cast_and_store(units[-3])
        matmuls(units[-2])
        gelus(units[-2])
        matmuls(units[-1])
        gelus(units[-1])
        finish_small(units[-2])
        finish_small(units[-1])
